import numpy as np
import ml_dtypes

BF16 = ml_dtypes.bfloat16


def bf(x):
    return np.asarray(x, np.float32).astype(BF16)


def f32(x):
    return np.asarray(x, np.float32)


def f64(x):
    return np.asarray(x).astype(np.float64)


def striped(idx):
    return np.tile(idx.reshape(-1, 16).T, (8, 1))


C, F, S, N = 256, 1024, 2048, 1024
EPS = 1e-5
ERF_TERMS = 150
ERF_LIMIT = 6.0


def erf(a):
    t = np.clip(a, -ERF_LIMIT, ERF_LIMIT)
    term = t.copy()
    total = t.copy()
    for n in range(1, ERF_TERMS):
        term = term * (2.0 * t * t) / (2.0 * n + 1.0)
        total = total + term
    v = 2.0 / np.sqrt(np.pi) * np.exp(-t * t) * total
    return np.where(np.abs(a) > ERF_LIMIT, np.sign(a), v)


def gelu(v):
    return 0.5 * v * (1.0 + erf(v / np.sqrt(2.0)))


def setup_inputs():
    return {"base": f32(np.random.standard_normal((C, S))), "h": f32(np.random.standard_normal((C, N))), "ln_gain": f32(1.0 + 0.1 * np.random.standard_normal((C, 1))), "ln_bias": f32(0.1 * np.random.standard_normal((C, 1))), "w1": bf(np.random.standard_normal((C, F)) / np.sqrt(C)), "b1": f32(0.1 * np.random.standard_normal((F, 1))), "w2": bf(np.random.standard_normal((F, C)) / np.sqrt(F)), "b2": f32(0.1 * np.random.standard_normal((C, 1))), "offs": striped(np.random.permutation(S)[:N])}


def reference(base, h, ln_gain, ln_bias, w1, b1, w2, b2, offs):
    idx = offs[:16].T.reshape(-1)
    hh = f64(h)
    mu = hh.mean(axis=0, keepdims=True)
    var = ((hh - mu) ** 2).mean(axis=0, keepdims=True)
    x = (hh - mu) / np.sqrt(var + EPS) * f64(ln_gain) + f64(ln_bias)
    a = gelu(f64(w1).T @ x + f64(b1))
    y = f64(w2).T @ a + f64(b2)
    out = f64(base).copy()
    out[:, idx] = hh + y
    return out

@@ -1,0 +1,158 @@
+import concourse.mybir as mybir
+from concourse.masks import make_identity
+
+F32 = mybir.dt.float32
+BF16 = mybir.dt.bfloat16
+U16 = mybir.dt.uint16
+ACT = mybir.ActivationFunctionType
+ALU = mybir.AluOpType
+
+P = 128
+C = 256
+F = 1024
+S = 2048
+N = 1024
+EPS = 1e-5
+BANK = 512
+
+C_BLOCKS = C // P
+F_BLOCKS = F // P
+TOKEN_TILES = N // P
+HALVES = N // BANK
+TILES_PER_HALF = BANK // P
+
+COL_B1 = 0
+COL_GAIN = COL_B1 + F_BLOCKS
+COL_BIAS = COL_GAIN + C_BLOCKS
+COL_B2 = COL_BIAS + C_BLOCKS
+COLS_USED = COL_B2 + C_BLOCKS
+
+FLOPS = 2 * C * F * N * 2
+
+
+def tile_multiheadefralayer_kernel(tc, base, h, ln_gain, ln_bias, w1, b1, w2, b2, offs, out):
+    nc = tc.nc
+    with (
+        tc.tile_pool(name="held", bufs=1) as held,
+        tc.psum_pool(name="banks", bufs=8) as banks,
+    ):
+        offsets = held.tile([P, N // 16], U16, name="offsets")
+        nc.sync.dma_start(offsets[:], offs)
+
+        queues = (nc.sync, nc.scalar)
+        h_sb = [held.tile([P, N], F32, name=f"h{blk}") for blk in range(C_BLOCKS)]
+        for half in range(HALVES):
+            for blk in range(C_BLOCKS):
+                queues[blk].dma_start(
+                    h_sb[blk][:, half * BANK : (half + 1) * BANK],
+                    h[blk * P : (blk + 1) * P, half * BANK : (half + 1) * BANK],
+                )
+
+        rows = held.tile([P, P], F32, name="rows")
+        nc.vector.memset(rows[:], 0.0)
+        for vector, first_row in ((b1, COL_B1), (ln_gain, COL_GAIN), (ln_bias, COL_BIAS), (b2, COL_B2)):
+            as_rows = vector.rearrange("(r p) one -> r (p one)", p=P)
+            nc.gpsimd.dma_start(rows[first_row : first_row + as_rows.shape[0], :], as_rows)
+
+        w1_sb = [held.tile([P, F], BF16, name=f"w1_{blk}") for blk in range(C_BLOCKS)]
+        for blk in range(C_BLOCKS):
+            queues[blk].dma_start(w1_sb[blk][:], w1[blk * P : (blk + 1) * P, :])
+        w2_sb = held.tile([P, F_BLOCKS, C], BF16, name="w2_sb")
+        nc.sync.dma_start(w2_sb[:], w2.rearrange("(k p) c -> p k c", p=P))
+        window = [held.tile([P, S], F32, name=f"window{blk}") for blk in range(C_BLOCKS)]
+        for blk in range(C_BLOCKS):
+            queues[blk].dma_start(window[blk][:], base[blk * P : (blk + 1) * P, :])
+
+        identity = held.tile([P, P], F32, name="identity")
+        make_identity(nc, identity[:])
+        eps = held.tile([P, 1], F32, name="eps")
+        nc.vector.memset(eps[:], EPS)
+
+        flipped_rows = banks.tile([P, BANK], F32, name="flipped_rows", tag="bank")
+        nc.tensor.transpose(flipped_rows[:, 0:P], rows[:], identity[:])
+        per_partition = held.tile([P, COLS_USED], F32, name="per_partition")
+        nc.vector.tensor_copy(per_partition[:], flipped_rows[:, 0:COLS_USED])
+
+        stats = held.tile([P, TOKEN_TILES, 6], F32, name="stats")
+        mean_var = held.tile([P, TOKEN_TILES, 2], F32, name="mean_var")
+        h_flipped = []
+        for pair in range(TOKEN_TILES // 2):
+            bank = banks.tile([P, 2, C], F32, name=f"h_flipped{pair}", tag="bank")
+            h_flipped.append(bank)
+            for side in range(2):
+                t = 2 * pair + side
+                for blk in range(C_BLOCKS):
+                    nc.tensor.transpose(
+                        bank[:, side, blk * P : (blk + 1) * P], h_sb[blk][:, t * P : (t + 1) * P], identity[:]
+                    )
+            for side in range(2):
+                t = 2 * pair + side
+                nc.vector.bn_stats(stats[:, t, :], bank[:, side, :])
+                nc.vector.bn_aggr(mean_var[:, t, :], stats[:, t, :])
+
+        std = held.tile([P, TOKEN_TILES, 1], F32, name="std")
+        nc.scalar.activation(std[:], mean_var[:, :, 1:2], ACT.Sqrt, bias=eps[:])
+        rstd = held.tile([P, TOKEN_TILES, 1], F32, name="rstd")
+        nc.vector.reciprocal(rstd[:], std[:])
+
+        normed = held.tile([P, TOKEN_TILES, C], F32, name="normed")
+        x_sb = [held.tile([P, N], BF16, name=f"x{blk}") for blk in range(C_BLOCKS)]
+        a_sb = held.tile([P, F_BLOCKS, N], BF16, name="a_sb")
+        for half in range(HALVES):
+            tokens = slice(half * BANK, (half + 1) * BANK)
+            back = [banks.tile([P, BANK], F32, name=f"back{half}_{blk}", tag="bank") for blk in range(C_BLOCKS)]
+            for q in range(TILES_PER_HALF):
+                t = half * TILES_PER_HALF + q
+                nc.vector.tensor_scalar(
+                    normed[:, t, :],
+                    h_flipped[t // 2][:, t % 2, :],
+                    mean_var[:, t, 0:1],
+                    rstd[:, t, :],
+                    ALU.subtract,
+                    ALU.mult,
+                )
+                for blk in range(C_BLOCKS):
+                    nc.tensor.transpose(
+                        back[blk][:, q * P : (q + 1) * P], normed[:, t, blk * P : (blk + 1) * P], identity[:]
+                    )
+            for blk in range(C_BLOCKS):
+                nc.vector.tensor_scalar(
+                    x_sb[blk][:, tokens],
+                    back[blk][:],
+                    per_partition[:, COL_GAIN + blk : COL_GAIN + blk + 1],
+                    per_partition[:, COL_BIAS + blk : COL_BIAS + blk + 1],
+                    ALU.mult,
+                    ALU.add,
+                )
+            for m in range(F_BLOCKS):
+                z = banks.tile([P, BANK], F32, name="z", tag="bank")
+                for k in range(C_BLOCKS):
+                    nc.tensor.matmul(
+                        z[:],
+                        w1_sb[k][:, m * P : (m + 1) * P],
+                        x_sb[k][:, tokens],
+                        start=(k == 0),
+                        stop=(k == C_BLOCKS - 1),
+                    )
+                nc.scalar.activation(
+                    a_sb[:, m, tokens], z[:], ACT.Gelu, bias=per_partition[:, COL_B1 + m : COL_B1 + m + 1]
+                )
+
+        y_sb = [held.tile([P, N], F32, name=f"y{blk}") for blk in range(C_BLOCKS)]
+        for blk in range(C_BLOCKS):
+            for half in range(HALVES):
+                tokens = slice(half * BANK, (half + 1) * BANK)
+                y = banks.tile([P, BANK], F32, name="y", tag="bank")
+                for k in range(F_BLOCKS):
+                    nc.tensor.matmul(
+                        y[:],
+                        w2_sb[:, k, blk * P : (blk + 1) * P],
+                        a_sb[:, k, tokens],
+                        start=(k == 0),
+                        stop=(k == F_BLOCKS - 1),
+                    )
+                nc.scalar.activation(
+                    y_sb[blk][:, tokens], y[:], ACT.Identity, bias=per_partition[:, COL_B2 + blk : COL_B2 + blk + 1]
+                )
+            nc.vector.tensor_tensor(window[blk][:].indirect(offsets[:]), h_sb[blk][:], y_sb[blk][:], ALU.add)
+            nc.sync.dma_start(out[blk * P : (blk + 1) * P, :], window[blk][:])

@@ -18,8 +18,11 @@ BANK = 512
 C_BLOCKS = C // P
 F_BLOCKS = F // P
 TOKEN_TILES = N // P
+GROUP = BANK * P // C
+GROUPS = N // GROUP
+TILES_PER_GROUP = GROUP // P
 HALVES = N // BANK
-TILES_PER_HALF = BANK // P
+GROUPS_PER_HALF = BANK // GROUP
 
 COL_B1 = 0
 COL_GAIN = COL_B1 + F_BLOCKS
@@ -36,95 +39,113 @@ def tile_multiheadefralayer_kernel(tc, base, h, ln_gain, ln_bias, w1, b1, w2, b2
         tc.tile_pool(name="held", bufs=1) as held,
         tc.psum_pool(name="banks", bufs=8) as banks,
     ):
-        offsets = held.tile([P, N // 16], U16, name="offsets")
-        nc.sync.dma_start(offsets[:], offs)
-
-        queues = (nc.sync, nc.scalar)
-        h_sb = [held.tile([P, N], F32, name=f"h{blk}") for blk in range(C_BLOCKS)]
-        for half in range(HALVES):
-            for blk in range(C_BLOCKS):
-                queues[blk].dma_start(
-                    h_sb[blk][:, half * BANK : (half + 1) * BANK],
-                    h[blk * P : (blk + 1) * P, half * BANK : (half + 1) * BANK],
-                )
-
-        rows = held.tile([P, P], F32, name="rows")
-        nc.vector.memset(rows[:], 0.0)
-        for vector, first_row in ((b1, COL_B1), (ln_gain, COL_GAIN), (ln_bias, COL_BIAS), (b2, COL_B2)):
-            as_rows = vector.rearrange("(r p) one -> r (p one)", p=P)
-            nc.gpsimd.dma_start(rows[first_row : first_row + as_rows.shape[0], :], as_rows)
-
-        w1_sb = [held.tile([P, F], BF16, name=f"w1_{blk}") for blk in range(C_BLOCKS)]
-        for blk in range(C_BLOCKS):
-            queues[blk].dma_start(w1_sb[blk][:], w1[blk * P : (blk + 1) * P, :])
-        w2_sb = held.tile([P, F_BLOCKS, C], BF16, name="w2_sb")
-        nc.sync.dma_start(w2_sb[:], w2.rearrange("(k p) c -> p k c", p=P))
-        window = [held.tile([P, S], F32, name=f"window{blk}") for blk in range(C_BLOCKS)]
-        for blk in range(C_BLOCKS):
-            queues[blk].dma_start(window[blk][:], base[blk * P : (blk + 1) * P, :])
-
         identity = held.tile([P, P], F32, name="identity")
         make_identity(nc, identity[:])
         eps = held.tile([P, 1], F32, name="eps")
         nc.vector.memset(eps[:], EPS)
+        rows = held.tile([P, P], F32, name="rows")
+        nc.vector.memset(rows[:], 0.0)
 
-        flipped_rows = banks.tile([P, BANK], F32, name="flipped_rows", tag="bank")
-        nc.tensor.transpose(flipped_rows[:, 0:P], rows[:], identity[:])
-        per_partition = held.tile([P, COLS_USED], F32, name="per_partition")
-        nc.vector.tensor_copy(per_partition[:], flipped_rows[:, 0:COLS_USED])
+        h_sb = [held.tile([P, N], F32, name=f"h{blk}") for blk in range(C_BLOCKS)]
 
-        stats = held.tile([P, TOKEN_TILES, 6], F32, name="stats")
-        mean_var = held.tile([P, TOKEN_TILES, 2], F32, name="mean_var")
-        h_flipped = []
-        for pair in range(TOKEN_TILES // 2):
-            bank = banks.tile([P, 2, C], F32, name=f"h_flipped{pair}", tag="bank")
-            h_flipped.append(bank)
-            for side in range(2):
-                t = 2 * pair + side
-                for blk in range(C_BLOCKS):
-                    nc.tensor.transpose(
-                        bank[:, side, blk * P : (blk + 1) * P], h_sb[blk][:, t * P : (t + 1) * P], identity[:]
-                    )
-            for side in range(2):
-                t = 2 * pair + side
-                nc.vector.bn_stats(stats[:, t, :], bank[:, side, :])
-                nc.vector.bn_aggr(mean_var[:, t, :], stats[:, t, :])
+        def load_h(group):
+            tokens = slice(group * GROUP, (group + 1) * GROUP)
+            for blk in range(C_BLOCKS):
+                nc.sync.dma_start(h_sb[blk][:, tokens], h[blk * P : (blk + 1) * P, tokens])
 
-        std = held.tile([P, TOKEN_TILES, 1], F32, name="std")
-        nc.scalar.activation(std[:], mean_var[:, :, 1:2], ACT.Sqrt, bias=eps[:])
-        rstd = held.tile([P, TOKEN_TILES, 1], F32, name="rstd")
-        nc.vector.reciprocal(rstd[:], std[:])
+        load_h(0)
+        load_h(1)
+        for vector, first_row in ((b1, COL_B1), (ln_gain, COL_GAIN), (ln_bias, COL_BIAS), (b2, COL_B2)):
+            as_rows = vector.rearrange("(r p) one -> r (p one)", p=P)
+            nc.sync.dma_start(rows[first_row : first_row + as_rows.shape[0], :], as_rows)
+        load_h(2)
+        load_h(3)
+        w1_sb = [held.tile([P, F], BF16, name=f"w1_{blk}") for blk in range(C_BLOCKS)]
+        for blk in range(C_BLOCKS):
+            nc.sync.dma_start(w1_sb[blk][:], w1[blk * P : (blk + 1) * P, :])
+        w2_sb = held.tile([P, F_BLOCKS, C], BF16, name="w2_sb")
+        nc.sync.dma_start(w2_sb[:], w2.rearrange("(k p) c -> p k c", p=P))
+        offsets = held.tile([P, N // 16], U16, name="offsets")
+        nc.sync.dma_start(offsets[:], offs)
+        window = [held.tile([P, S], F32, name=f"window{blk}") for blk in range(C_BLOCKS)]
+        for blk in range(C_BLOCKS):
+            nc.sync.dma_start(window[blk][:], base[blk * P : (blk + 1) * P, :])
 
+        table_warmer = held.tile([P, 1], F32, name="table_warmer")
+        nc.scalar.activation(table_warmer[:], eps[:], ACT.Sqrt)
+
+        stats = [held.tile([P, TILES_PER_GROUP, 6], F32, name=f"stats{g}") for g in range(GROUPS)]
+        mean_var = [held.tile([P, TILES_PER_GROUP, 2], F32, name=f"mean_var{g}") for g in range(GROUPS)]
+        neg_mean = [held.tile([P, TILES_PER_GROUP, 1], F32, name=f"neg_mean{g}") for g in range(GROUPS)]
+        std = [held.tile([P, TILES_PER_GROUP, 1], F32, name=f"std{g}") for g in range(GROUPS)]
+        rstd = [held.tile([P, TILES_PER_GROUP, 1], F32, name=f"rstd{g}") for g in range(GROUPS)]
+        shift = [held.tile([P, TILES_PER_GROUP, 1], F32, name=f"shift{g}") for g in range(GROUPS)]
         normed = held.tile([P, TOKEN_TILES, C], F32, name="normed")
+        per_partition = held.tile([P, COLS_USED], F32, name="per_partition")
         x_sb = [held.tile([P, N], BF16, name=f"x{blk}") for blk in range(C_BLOCKS)]
         a_sb = held.tile([P, F_BLOCKS, N], BF16, name="a_sb")
-        for half in range(HALVES):
-            tokens = slice(half * BANK, (half + 1) * BANK)
-            back = [banks.tile([P, BANK], F32, name=f"back{half}_{blk}", tag="bank") for blk in range(C_BLOCKS)]
-            for q in range(TILES_PER_HALF):
-                t = half * TILES_PER_HALF + q
-                nc.vector.tensor_scalar(
-                    normed[:, t, :],
-                    h_flipped[t // 2][:, t % 2, :],
-                    mean_var[:, t, 0:1],
-                    rstd[:, t, :],
-                    ALU.subtract,
-                    ALU.mult,
+        h_flipped = {}
+        back = {}
+
+        def scale_and_shift(engine, result, data, scale, offset):
+            if engine == "scalar":
+                nc.scalar.activation(result, data, ACT.Identity, bias=offset, scale=scale)
+            else:
+                nc.vector.tensor_scalar(result, data, scale, offset, ALU.mult, ALU.add)
+
+        def flip_small_vectors():
+            flipped_rows = banks.tile([P, BANK], F32, name="flipped_rows", tag="bank")
+            nc.tensor.transpose(flipped_rows[:, 0:P], rows[:], identity[:])
+            nc.vector.tensor_copy(per_partition[:], flipped_rows[:, 0:COLS_USED])
+
+        def moments(group):
+            h_flipped[group] = banks.tile([P, TILES_PER_GROUP, C], F32, name=f"h_flipped{group}", tag="bank")
+            for i in range(TILES_PER_GROUP):
+                t = group * TILES_PER_GROUP + i
+                for blk in range(C_BLOCKS):
+                    nc.tensor.transpose(
+                        h_flipped[group][:, i, blk * P : (blk + 1) * P], h_sb[blk][:, t * P : (t + 1) * P], identity[:]
+                    )
+            for i in range(TILES_PER_GROUP):
+                nc.vector.bn_stats(stats[group][:, i, :], h_flipped[group][:, i, :])
+            for i in range(TILES_PER_GROUP):
+                nc.vector.bn_aggr(mean_var[group][:, i, :], stats[group][:, i, :])
+            nc.vector.tensor_scalar_mul(neg_mean[group][:], mean_var[group][:, :, 0:1], -1.0)
+
+        def inverse_std(group):
+            nc.scalar.activation(std[group][:], mean_var[group][:, :, 1:2], ACT.Sqrt, bias=eps[:])
+            nc.vector.reciprocal(rstd[group][:], std[group][:])
+            nc.vector.tensor_tensor(shift[group][:], neg_mean[group][:], rstd[group][:], ALU.mult)
+
+        def normalise(group, engine):
+            half = group // GROUPS_PER_HALF
+            if group % GROUPS_PER_HALF == 0:
+                for blk in range(C_BLOCKS):
+                    back[half, blk] = banks.tile([P, BANK], F32, name=f"back{half}_{blk}", tag="bank")
+            for i in range(TILES_PER_GROUP):
+                t = group * TILES_PER_GROUP + i
+                column = t * P - half * BANK
+                scale_and_shift(
+                    engine, normed[:, t, :], h_flipped[group][:, i, :], rstd[group][:, i, :], shift[group][:, i, :]
                 )
                 for blk in range(C_BLOCKS):
                     nc.tensor.transpose(
-                        back[blk][:, q * P : (q + 1) * P], normed[:, t, blk * P : (blk + 1) * P], identity[:]
+                        back[half, blk][:, column : column + P], normed[:, t, blk * P : (blk + 1) * P], identity[:]
                     )
+
+        def gain_and_bias(half, engines):
             for blk in range(C_BLOCKS):
-                nc.vector.tensor_scalar(
-                    x_sb[blk][:, tokens],
-                    back[blk][:],
+                scale_and_shift(
+                    engines[blk],
+                    x_sb[blk][:, half * BANK : (half + 1) * BANK],
+                    back[half, blk][:],
                     per_partition[:, COL_GAIN + blk : COL_GAIN + blk + 1],
                     per_partition[:, COL_BIAS + blk : COL_BIAS + blk + 1],
-                    ALU.mult,
-                    ALU.add,
                 )
-            for m in range(F_BLOCKS):
+
+        def first_matmul(half, feature_blocks):
+            tokens = slice(half * BANK, (half + 1) * BANK)
+            for m in feature_blocks:
                 z = banks.tile([P, BANK], F32, name="z", tag="bank")
                 for k in range(C_BLOCKS):
                     nc.tensor.matmul(
@@ -137,6 +158,25 @@ def tile_multiheadefralayer_kernel(tc, base, h, ln_gain, ln_bias, w1, b1, w2, b2
                 nc.scalar.activation(
                     a_sb[:, m, tokens], z[:], ACT.Gelu, bias=per_partition[:, COL_B1 + m : COL_B1 + m + 1]
                 )
+
+        moments(0)
+        moments(1)
+        inverse_std(0)
+        inverse_std(1)
+        flip_small_vectors()
+        moments(2)
+        moments(3)
+        normalise(0, "scalar")
+        normalise(1, "scalar")
+        gain_and_bias(0, ("scalar", "vector"))
+        inverse_std(2)
+        inverse_std(3)
+        first_matmul(0, range(0, F_BLOCKS // 2))
+        normalise(2, "vector")
+        normalise(3, "vector")
+        gain_and_bias(1, ("vector", "vector"))
+        first_matmul(0, range(F_BLOCKS // 2, F_BLOCKS))
+        first_matmul(1, range(F_BLOCKS))
 
         y_sb = [held.tile([P, N], F32, name=f"y{blk}") for blk in range(C_BLOCKS)]
         for blk in range(C_BLOCKS):

@@ -45,6 +45,8 @@ def tile_multiheadefralayer_kernel(tc, base, h, ln_gain, ln_bias, w1, b1, w2, b2
         nc.vector.memset(eps[:], EPS)
         rows = held.tile([P, P], F32, name="rows")
         nc.vector.memset(rows[:], 0.0)
+        zeros = held.tile([P, BANK], BF16, name="zeros")
+        nc.vector.memset(zeros[:], 0.0)
 
         h_sb = [held.tile([P, N], F32, name=f"h{blk}") for blk in range(C_BLOCKS)]
 
@@ -86,6 +88,12 @@ def tile_multiheadefralayer_kernel(tc, base, h, ln_gain, ln_bias, w1, b1, w2, b2
         a_sb = held.tile([P, F_BLOCKS, N], BF16, name="a_sb")
         h_flipped = {}
         back = {}
+
+        unread = banks.tile([P, BANK], F32, name="unread", tag="bank")
+
+        def keep_clock_up(matmuls):
+            for i in range(matmuls):
+                nc.tensor.matmul(unread[:], zeros[:, 0:P], zeros[:], start=True, stop=True)
 
         def scale_and_shift(engine, result, data, scale, offset):
             if engine == "scalar":
@@ -159,15 +167,22 @@ def tile_multiheadefralayer_kernel(tc, base, h, ln_gain, ln_bias, w1, b1, w2, b2
                     a_sb[:, m, tokens], z[:], ACT.Gelu, bias=per_partition[:, COL_B1 + m : COL_B1 + m + 1]
                 )
 
+        keep_clock_up(4)
         moments(0)
+        keep_clock_up(1)
         moments(1)
+        keep_clock_up(1)
         inverse_std(0)
         inverse_std(1)
         flip_small_vectors()
         moments(2)
+        keep_clock_up(1)
         moments(3)
+        keep_clock_up(1)
         normalise(0, "scalar")
+        keep_clock_up(1)
         normalise(1, "scalar")
+        keep_clock_up(1)
         gain_and_bias(0, ("scalar", "vector"))
         inverse_std(2)
         inverse_std(3)

@@ -45,8 +45,6 @@ def tile_multiheadefralayer_kernel(tc, base, h, ln_gain, ln_bias, w1, b1, w2, b2
         nc.vector.memset(eps[:], EPS)
         rows = held.tile([P, P], F32, name="rows")
         nc.vector.memset(rows[:], 0.0)
-        zeros = held.tile([P, BANK], BF16, name="zeros")
-        nc.vector.memset(zeros[:], 0.0)
 
         h_sb = [held.tile([P, N], F32, name=f"h{blk}") for blk in range(C_BLOCKS)]
 
@@ -78,10 +76,10 @@ def tile_multiheadefralayer_kernel(tc, base, h, ln_gain, ln_bias, w1, b1, w2, b2
 
         stats = [held.tile([P, TILES_PER_GROUP, 6], F32, name=f"stats{g}") for g in range(GROUPS)]
         mean_var = [held.tile([P, TILES_PER_GROUP, 2], F32, name=f"mean_var{g}") for g in range(GROUPS)]
-        neg_mean = [held.tile([P, TILES_PER_GROUP, 1], F32, name=f"neg_mean{g}") for g in range(GROUPS)]
         std = [held.tile([P, TILES_PER_GROUP, 1], F32, name=f"std{g}") for g in range(GROUPS)]
         rstd = [held.tile([P, TILES_PER_GROUP, 1], F32, name=f"rstd{g}") for g in range(GROUPS)]
-        shift = [held.tile([P, TILES_PER_GROUP, 1], F32, name=f"shift{g}") for g in range(GROUPS)]
+        neg_mean = held.tile([P, TILES_PER_GROUP, 1], F32, name="neg_mean")
+        shift = held.tile([P, TILES_PER_GROUP, 1], F32, name="shift")
         normed = held.tile([P, TOKEN_TILES, C], F32, name="normed")
         per_partition = held.tile([P, COLS_USED], F32, name="per_partition")
         x_sb = [held.tile([P, N], BF16, name=f"x{blk}") for blk in range(C_BLOCKS)]
@@ -89,24 +87,12 @@ def tile_multiheadefralayer_kernel(tc, base, h, ln_gain, ln_bias, w1, b1, w2, b2
         h_flipped = {}
         back = {}
 
-        unread = banks.tile([P, BANK], F32, name="unread", tag="bank")
-
-        def keep_clock_up(matmuls):
-            for i in range(matmuls):
-                nc.tensor.matmul(unread[:], zeros[:, 0:P], zeros[:], start=True, stop=True)
-
-        def scale_and_shift(engine, result, data, scale, offset):
-            if engine == "scalar":
-                nc.scalar.activation(result, data, ACT.Identity, bias=offset, scale=scale)
-            else:
-                nc.vector.tensor_scalar(result, data, scale, offset, ALU.mult, ALU.add)
-
         def flip_small_vectors():
             flipped_rows = banks.tile([P, BANK], F32, name="flipped_rows", tag="bank")
             nc.tensor.transpose(flipped_rows[:, 0:P], rows[:], identity[:])
-            nc.vector.tensor_copy(per_partition[:], flipped_rows[:, 0:COLS_USED])
+            nc.scalar.copy(per_partition[:], flipped_rows[:, 0:COLS_USED])
 
-        def moments(group):
+        def flip_in(group):
             h_flipped[group] = banks.tile([P, TILES_PER_GROUP, C], F32, name=f"h_flipped{group}", tag="bank")
             for i in range(TILES_PER_GROUP):
                 t = group * TILES_PER_GROUP + i
@@ -114,18 +100,21 @@ def tile_multiheadefralayer_kernel(tc, base, h, ln_gain, ln_bias, w1, b1, w2, b2
                     nc.tensor.transpose(
                         h_flipped[group][:, i, blk * P : (blk + 1) * P], h_sb[blk][:, t * P : (t + 1) * P], identity[:]
                     )
+
+        def moments(group):
             for i in range(TILES_PER_GROUP):
                 nc.vector.bn_stats(stats[group][:, i, :], h_flipped[group][:, i, :])
             for i in range(TILES_PER_GROUP):
                 nc.vector.bn_aggr(mean_var[group][:, i, :], stats[group][:, i, :])
-            nc.vector.tensor_scalar_mul(neg_mean[group][:], mean_var[group][:, :, 0:1], -1.0)
 
         def inverse_std(group):
             nc.scalar.activation(std[group][:], mean_var[group][:, :, 1:2], ACT.Sqrt, bias=eps[:])
             nc.vector.reciprocal(rstd[group][:], std[group][:])
-            nc.vector.tensor_tensor(shift[group][:], neg_mean[group][:], rstd[group][:], ALU.mult)
 
         def normalise(group, engine):
+            if engine == "scalar":
+                nc.gpsimd.tensor_scalar_mul(neg_mean[:], mean_var[group][:, :, 0:1], -1.0)
+                nc.gpsimd.tensor_tensor(shift[:], neg_mean[:], rstd[group][:], ALU.mult)
             half = group // GROUPS_PER_HALF
             if group % GROUPS_PER_HALF == 0:
                 for blk in range(C_BLOCKS):
@@ -133,23 +122,33 @@ def tile_multiheadefralayer_kernel(tc, base, h, ln_gain, ln_bias, w1, b1, w2, b2
             for i in range(TILES_PER_GROUP):
                 t = group * TILES_PER_GROUP + i
                 column = t * P - half * BANK
-                scale_and_shift(
-                    engine, normed[:, t, :], h_flipped[group][:, i, :], rstd[group][:, i, :], shift[group][:, i, :]
-                )
+                if engine == "scalar":
+                    nc.scalar.activation(
+                        normed[:, t, :], h_flipped[group][:, i, :], ACT.Identity, bias=shift[:, i, :], scale=rstd[group][:, i, :]
+                    )
+                else:
+                    nc.vector.tensor_scalar(
+                        normed[:, t, :],
+                        h_flipped[group][:, i, :],
+                        mean_var[group][:, i, 0:1],
+                        rstd[group][:, i, :],
+                        ALU.subtract,
+                        ALU.mult,
+                    )
                 for blk in range(C_BLOCKS):
                     nc.tensor.transpose(
                         back[half, blk][:, column : column + P], normed[:, t, blk * P : (blk + 1) * P], identity[:]
                     )
 
-        def gain_and_bias(half, engines):
+        def gain_and_bias(half, engine):
             for blk in range(C_BLOCKS):
-                scale_and_shift(
-                    engines[blk],
-                    x_sb[blk][:, half * BANK : (half + 1) * BANK],
-                    back[half, blk][:],
-                    per_partition[:, COL_GAIN + blk : COL_GAIN + blk + 1],
-                    per_partition[:, COL_BIAS + blk : COL_BIAS + blk + 1],
-                )
+                x_half = x_sb[blk][:, half * BANK : (half + 1) * BANK]
+                gain = per_partition[:, COL_GAIN + blk : COL_GAIN + blk + 1]
+                bias = per_partition[:, COL_BIAS + blk : COL_BIAS + blk + 1]
+                if engine == "scalar":
+                    nc.scalar.activation(x_half, back[half, blk][:], ACT.Identity, bias=bias, scale=gain)
+                else:
+                    nc.vector.tensor_scalar(x_half, back[half, blk][:], gain, bias, ALU.mult, ALU.add)
 
         def first_matmul(half, feature_blocks):
             tokens = slice(half * BANK, (half + 1) * BANK)
@@ -167,29 +166,26 @@ def tile_multiheadefralayer_kernel(tc, base, h, ln_gain, ln_bias, w1, b1, w2, b2
                     a_sb[:, m, tokens], z[:], ACT.Gelu, bias=per_partition[:, COL_B1 + m : COL_B1 + m + 1]
                 )
 
-        keep_clock_up(4)
+        flip_in(0)
         moments(0)
-        keep_clock_up(1)
+        flip_in(1)
         moments(1)
-        keep_clock_up(1)
         inverse_std(0)
         inverse_std(1)
         flip_small_vectors()
-        moments(2)
-        keep_clock_up(1)
-        moments(3)
-        keep_clock_up(1)
+        flip_in(2)
+        flip_in(3)
         normalise(0, "scalar")
-        keep_clock_up(1)
-        normalise(1, "scalar")
-        keep_clock_up(1)
-        gain_and_bias(0, ("scalar", "vector"))
+        normalise(1, "vector")
+        moments(2)
+        moments(3)
+        gain_and_bias(0, "scalar")
         inverse_std(2)
         inverse_std(3)
         first_matmul(0, range(0, F_BLOCKS // 2))
         normalise(2, "vector")
         normalise(3, "vector")
-        gain_and_bias(1, ("vector", "vector"))
+        gain_and_bias(1, "vector")
         first_matmul(0, range(F_BLOCKS // 2, F_BLOCKS))
         first_matmul(1, range(F_BLOCKS))
 

@@ -152,19 +152,21 @@ def tile_multiheadefralayer_kernel(tc, base, h, ln_gain, ln_bias, w1, b1, w2, b2
 
         def first_matmul(half, feature_blocks):
             tokens = slice(half * BANK, (half + 1) * BANK)
-            for m in feature_blocks:
-                z = banks.tile([P, BANK], F32, name="z", tag="bank")
+            for pair in zip(feature_blocks[0::2], feature_blocks[1::2]):
+                z = {m: banks.tile([P, BANK], F32, name=f"z{m % 2}", tag="bank") for m in pair}
                 for k in range(C_BLOCKS):
-                    nc.tensor.matmul(
-                        z[:],
-                        w1_sb[k][:, m * P : (m + 1) * P],
-                        x_sb[k][:, tokens],
-                        start=(k == 0),
-                        stop=(k == C_BLOCKS - 1),
+                    for m in pair:
+                        nc.tensor.matmul(
+                            z[m][:],
+                            w1_sb[k][:, m * P : (m + 1) * P],
+                            x_sb[k][:, tokens],
+                            start=(k == 0),
+                            stop=(k == C_BLOCKS - 1),
+                        )
+                for m in pair:
+                    nc.scalar.activation(
+                        a_sb[:, m, tokens], z[m][:], ACT.Gelu, bias=per_partition[:, COL_B1 + m : COL_B1 + m + 1]
                     )
-                nc.scalar.activation(
-                    a_sb[:, m, tokens], z[:], ACT.Gelu, bias=per_partition[:, COL_B1 + m : COL_B1 + m + 1]
-                )
 
         flip_in(0)
         moments(0)

@@ -18,11 +18,9 @@ BANK = 512
 C_BLOCKS = C // P
 F_BLOCKS = F // P
 TOKEN_TILES = N // P
-GROUP = BANK * P // C
-GROUPS = N // GROUP
-TILES_PER_GROUP = GROUP // P
 HALVES = N // BANK
-GROUPS_PER_HALF = BANK // GROUP
+CHUNKS = ((0, 128), (128, 128), (256, 256), (512, 256), (768, 256))
+MAX_TILES = 2
 
 COL_B1 = 0
 COL_GAIN = COL_B1 + F_BLOCKS
@@ -41,25 +39,26 @@ def tile_multiheadefralayer_kernel(tc, base, h, ln_gain, ln_bias, w1, b1, w2, b2
     ):
         identity = held.tile([P, P], F32, name="identity")
         make_identity(nc, identity[:])
-        eps = held.tile([P, 1], F32, name="eps")
-        nc.vector.memset(eps[:], EPS)
+        minus_half = held.tile([P, MAX_TILES, 1], F32, name="minus_half")
+        nc.vector.memset(minus_half[:], -0.5)
         rows = held.tile([P, P], F32, name="rows")
         nc.vector.memset(rows[:], 0.0)
 
         h_sb = [held.tile([P, N], F32, name=f"h{blk}") for blk in range(C_BLOCKS)]
 
-        def load_h(group):
-            tokens = slice(group * GROUP, (group + 1) * GROUP)
+        def load_h(chunk):
+            first, size = CHUNKS[chunk]
             for blk in range(C_BLOCKS):
-                nc.sync.dma_start(h_sb[blk][:, tokens], h[blk * P : (blk + 1) * P, tokens])
+                nc.sync.dma_start(h_sb[blk][:, first : first + size], h[blk * P : (blk + 1) * P, first : first + size])
 
         load_h(0)
         load_h(1)
+        load_h(2)
         for vector, first_row in ((b1, COL_B1), (ln_gain, COL_GAIN), (ln_bias, COL_BIAS), (b2, COL_B2)):
             as_rows = vector.rearrange("(r p) one -> r (p one)", p=P)
             nc.sync.dma_start(rows[first_row : first_row + as_rows.shape[0], :], as_rows)
-        load_h(2)
         load_h(3)
+        load_h(4)
         w1_sb = [held.tile([P, F], BF16, name=f"w1_{blk}") for blk in range(C_BLOCKS)]
         for blk in range(C_BLOCKS):
             nc.sync.dma_start(w1_sb[blk][:], w1[blk * P : (blk + 1) * P, :])
@@ -72,14 +71,13 @@ def tile_multiheadefralayer_kernel(tc, base, h, ln_gain, ln_bias, w1, b1, w2, b2
             nc.sync.dma_start(window[blk][:], base[blk * P : (blk + 1) * P, :])
 
         table_warmer = held.tile([P, 1], F32, name="table_warmer")
-        nc.scalar.activation(table_warmer[:], eps[:], ACT.Sqrt)
+        nc.scalar.activation(table_warmer[:], minus_half[:, 0, :], ACT.Gelu)
 
-        stats = [held.tile([P, TILES_PER_GROUP, 6], F32, name=f"stats{g}") for g in range(GROUPS)]
-        mean_var = [held.tile([P, TILES_PER_GROUP, 2], F32, name=f"mean_var{g}") for g in range(GROUPS)]
-        std = [held.tile([P, TILES_PER_GROUP, 1], F32, name=f"std{g}") for g in range(GROUPS)]
-        rstd = [held.tile([P, TILES_PER_GROUP, 1], F32, name=f"rstd{g}") for g in range(GROUPS)]
-        neg_mean = held.tile([P, TILES_PER_GROUP, 1], F32, name="neg_mean")
-        shift = held.tile([P, TILES_PER_GROUP, 1], F32, name="shift")
+        tiles_of = [size // P for first, size in CHUNKS]
+        stats = [held.tile([P, tiles, 6], F32, name=f"stats{c}") for c, tiles in enumerate(tiles_of)]
+        mean_var = [held.tile([P, tiles, 2], F32, name=f"mean_var{c}") for c, tiles in enumerate(tiles_of)]
+        var_eps = [held.tile([P, tiles, 1], F32, name=f"var_eps{c}") for c, tiles in enumerate(tiles_of)]
+        rstd = [held.tile([P, tiles, 1], F32, name=f"rstd{c}") for c, tiles in enumerate(tiles_of)]
         normed = held.tile([P, TOKEN_TILES, C], F32, name="normed")
         per_partition = held.tile([P, COLS_USED], F32, name="per_partition")
         x_sb = [held.tile([P, N], BF16, name=f"x{blk}") for blk in range(C_BLOCKS)]
@@ -92,104 +90,105 @@ def tile_multiheadefralayer_kernel(tc, base, h, ln_gain, ln_bias, w1, b1, w2, b2
             nc.tensor.transpose(flipped_rows[:, 0:P], rows[:], identity[:])
             nc.scalar.copy(per_partition[:], flipped_rows[:, 0:COLS_USED])
 
-        def flip_in(group):
-            h_flipped[group] = banks.tile([P, TILES_PER_GROUP, C], F32, name=f"h_flipped{group}", tag="bank")
-            for i in range(TILES_PER_GROUP):
-                t = group * TILES_PER_GROUP + i
+        def flip_in(chunk):
+            first, size = CHUNKS[chunk]
+            h_flipped[chunk] = banks.tile([P, tiles_of[chunk], C], F32, name=f"h_flipped{chunk}", tag="bank")
+            for i in range(tiles_of[chunk]):
+                tokens = slice(first + i * P, first + (i + 1) * P)
+                for blk in range(C_BLOCKS):
+                    nc.tensor.transpose(h_flipped[chunk][:, i, blk * P : (blk + 1) * P], h_sb[blk][:, tokens], identity[:])
+
+        def moments(chunk):
+            for i in range(tiles_of[chunk]):
+                nc.vector.bn_stats(stats[chunk][:, i, :], h_flipped[chunk][:, i, :])
+            for i in range(tiles_of[chunk]):
+                nc.vector.bn_aggr(mean_var[chunk][:, i, :], stats[chunk][:, i, :])
+            nc.vector.tensor_scalar_add(var_eps[chunk][:], mean_var[chunk][:, :, 1:2], EPS)
+            nc.gpsimd.tensor_tensor(rstd[chunk][:], var_eps[chunk][:], minus_half[:, 0 : tiles_of[chunk], :], ALU.pow)
+
+        def normalise(chunk):
+            first, size = CHUNKS[chunk]
+            back[chunk] = banks.tile([P, C_BLOCKS, size], F32, name=f"back{chunk}", tag="bank")
+            for i in range(tiles_of[chunk]):
+                t = first // P + i
+                nc.vector.tensor_scalar(
+                    normed[:, t, :],
+                    h_flipped[chunk][:, i, :],
+                    mean_var[chunk][:, i, 0:1],
+                    rstd[chunk][:, i, :],
+                    ALU.subtract,
+                    ALU.mult,
+                )
                 for blk in range(C_BLOCKS):
                     nc.tensor.transpose(
-                        h_flipped[group][:, i, blk * P : (blk + 1) * P], h_sb[blk][:, t * P : (t + 1) * P], identity[:]
+                        back[chunk][:, blk, i * P : (i + 1) * P], normed[:, t, blk * P : (blk + 1) * P], identity[:]
                     )
 
-        def moments(group):
-            for i in range(TILES_PER_GROUP):
-                nc.vector.bn_stats(stats[group][:, i, :], h_flipped[group][:, i, :])
-            for i in range(TILES_PER_GROUP):
-                nc.vector.bn_aggr(mean_var[group][:, i, :], stats[group][:, i, :])
-
-        def inverse_std(group):
-            nc.scalar.activation(std[group][:], mean_var[group][:, :, 1:2], ACT.Sqrt, bias=eps[:])
-            nc.vector.reciprocal(rstd[group][:], std[group][:])
-
-        def normalise(group, engine):
-            if engine == "scalar":
-                nc.gpsimd.tensor_scalar_mul(neg_mean[:], mean_var[group][:, :, 0:1], -1.0)
-                nc.gpsimd.tensor_tensor(shift[:], neg_mean[:], rstd[group][:], ALU.mult)
-            half = group // GROUPS_PER_HALF
-            if group % GROUPS_PER_HALF == 0:
-                for blk in range(C_BLOCKS):
-                    back[half, blk] = banks.tile([P, BANK], F32, name=f"back{half}_{blk}", tag="bank")
-            for i in range(TILES_PER_GROUP):
-                t = group * TILES_PER_GROUP + i
-                column = t * P - half * BANK
-                if engine == "scalar":
-                    nc.scalar.activation(
-                        normed[:, t, :], h_flipped[group][:, i, :], ACT.Identity, bias=shift[:, i, :], scale=rstd[group][:, i, :]
-                    )
-                else:
-                    nc.vector.tensor_scalar(
-                        normed[:, t, :],
-                        h_flipped[group][:, i, :],
-                        mean_var[group][:, i, 0:1],
-                        rstd[group][:, i, :],
-                        ALU.subtract,
-                        ALU.mult,
-                    )
-                for blk in range(C_BLOCKS):
-                    nc.tensor.transpose(
-                        back[half, blk][:, column : column + P], normed[:, t, blk * P : (blk + 1) * P], identity[:]
-                    )
-
-        def gain_and_bias(half, engine):
+        def gain_and_bias(chunk, engine):
+            first, size = CHUNKS[chunk]
             for blk in range(C_BLOCKS):
-                x_half = x_sb[blk][:, half * BANK : (half + 1) * BANK]
+                x_chunk = x_sb[blk][:, first : first + size]
                 gain = per_partition[:, COL_GAIN + blk : COL_GAIN + blk + 1]
                 bias = per_partition[:, COL_BIAS + blk : COL_BIAS + blk + 1]
                 if engine == "scalar":
-                    nc.scalar.activation(x_half, back[half, blk][:], ACT.Identity, bias=bias, scale=gain)
+                    nc.scalar.activation(x_chunk, back[chunk][:, blk, :], ACT.Identity, bias=bias, scale=gain)
                 else:
-                    nc.vector.tensor_scalar(x_half, back[half, blk][:], gain, bias, ALU.mult, ALU.add)
+                    nc.vector.tensor_scalar(x_chunk, back[chunk][:, blk, :], gain, bias, ALU.mult, ALU.add)
 
-        def first_matmul(half, feature_blocks):
-            tokens = slice(half * BANK, (half + 1) * BANK)
-            for pair in zip(feature_blocks[0::2], feature_blocks[1::2]):
-                z = {m: banks.tile([P, BANK], F32, name=f"z{m % 2}", tag="bank") for m in pair}
-                for k in range(C_BLOCKS):
-                    for m in pair:
+        def first_matmul(chunk, feature_blocks):
+            first, size = CHUNKS[chunk]
+            tokens = slice(first, first + size)
+            per_bank = BANK // size
+            for lowest in feature_blocks[0::per_bank]:
+                z = banks.tile([P, per_bank, size], F32, name="z", tag="bank")
+                for i in range(per_bank):
+                    for k in range(C_BLOCKS):
                         nc.tensor.matmul(
-                            z[m][:],
-                            w1_sb[k][:, m * P : (m + 1) * P],
+                            z[:, i, :],
+                            w1_sb[k][:, (lowest + i) * P : (lowest + i + 1) * P],
                             x_sb[k][:, tokens],
                             start=(k == 0),
                             stop=(k == C_BLOCKS - 1),
                         )
-                for m in pair:
+                for i in range(per_bank):
+                    m = lowest + i
                     nc.scalar.activation(
-                        a_sb[:, m, tokens], z[m][:], ACT.Gelu, bias=per_partition[:, COL_B1 + m : COL_B1 + m + 1]
+                        a_sb[:, m, tokens], z[:, i, :], ACT.Gelu, bias=per_partition[:, COL_B1 + m : COL_B1 + m + 1]
                     )
 
+        lower = range(0, F_BLOCKS // 2)
+        upper = range(F_BLOCKS // 2, F_BLOCKS)
         flip_in(0)
         moments(0)
         flip_in(1)
         moments(1)
-        inverse_std(0)
-        inverse_std(1)
-        flip_small_vectors()
         flip_in(2)
-        flip_in(3)
-        normalise(0, "scalar")
-        normalise(1, "vector")
         moments(2)
-        moments(3)
+        flip_small_vectors()
+        flip_in(3)
+        flip_in(4)
+        normalise(0)
+        normalise(1)
         gain_and_bias(0, "scalar")
-        inverse_std(2)
-        inverse_std(3)
-        first_matmul(0, range(0, F_BLOCKS // 2))
-        normalise(2, "vector")
-        normalise(3, "vector")
-        gain_and_bias(1, "vector")
-        first_matmul(0, range(F_BLOCKS // 2, F_BLOCKS))
-        first_matmul(1, range(F_BLOCKS))
+        gain_and_bias(1, "scalar")
+        first_matmul(0, lower)
+        normalise(2)
+        first_matmul(0, upper)
+        moments(3)
+        gain_and_bias(2, "vector")
+        first_matmul(1, lower)
+        first_matmul(1, upper)
+        moments(4)
+        first_matmul(2, lower)
+        normalise(3)
+        first_matmul(2, upper)
+        normalise(4)
+        gain_and_bias(3, "vector")
+        gain_and_bias(4, "vector")
+        first_matmul(3, lower)
+        first_matmul(3, upper)
+        first_matmul(4, lower)
+        first_matmul(4, upper)
 
         y_sb = [held.tile([P, N], F32, name=f"y{blk}") for blk in range(C_BLOCKS)]
         for blk in range(C_BLOCKS):

@@ -18,7 +18,7 @@ BANK = 512
 C_BLOCKS = C // P
 F_BLOCKS = F // P
 TOKEN_TILES = N // P
-HALVES = N // BANK
+Y_PIECE = 256
 CHUNKS = ((0, 128), (128, 128), (256, 256), (512, 256), (768, 256))
 MAX_TILES = 2
 
@@ -192,9 +192,9 @@ def tile_multiheadefralayer_kernel(tc, base, h, ln_gain, ln_bias, w1, b1, w2, b2
 
         y_sb = [held.tile([P, N], F32, name=f"y{blk}") for blk in range(C_BLOCKS)]
         for blk in range(C_BLOCKS):
-            for half in range(HALVES):
-                tokens = slice(half * BANK, (half + 1) * BANK)
-                y = banks.tile([P, BANK], F32, name="y", tag="bank")
+            for piece in range(N // Y_PIECE):
+                tokens = slice(piece * Y_PIECE, (piece + 1) * Y_PIECE)
+                y = banks.tile([P, Y_PIECE], F32, name="y", tag="bank")
                 for k in range(F_BLOCKS):
                     nc.tensor.matmul(
                         y[:],

@@ -41,6 +41,8 @@ def tile_multiheadefralayer_kernel(tc, base, h, ln_gain, ln_bias, w1, b1, w2, b2
         make_identity(nc, identity[:])
         minus_half = held.tile([P, MAX_TILES, 1], F32, name="minus_half")
         nc.vector.memset(minus_half[:], -0.5)
+        eps = held.tile([P, 1], F32, name="eps")
+        nc.vector.memset(eps[:], EPS)
         rows = held.tile([P, P], F32, name="rows")
         nc.vector.memset(rows[:], 0.0)
 
@@ -70,13 +72,15 @@ def tile_multiheadefralayer_kernel(tc, base, h, ln_gain, ln_bias, w1, b1, w2, b2
         for blk in range(C_BLOCKS):
             nc.sync.dma_start(window[blk][:], base[blk * P : (blk + 1) * P, :])
 
-        table_warmer = held.tile([P, 1], F32, name="table_warmer")
-        nc.scalar.activation(table_warmer[:], minus_half[:, 0, :], ACT.Gelu)
+        table_warmer = held.tile([P, 2], F32, name="table_warmer")
+        nc.scalar.activation(table_warmer[:, 0:1], eps[:], ACT.Abs_reciprocal_sqrt)
+
+        def change_to_gelu_table(last_root):
+            nc.scalar.activation(table_warmer[:, 1:2], last_root, ACT.Gelu)
 
         tiles_of = [size // P for first, size in CHUNKS]
         stats = [held.tile([P, tiles, 6], F32, name=f"stats{c}") for c, tiles in enumerate(tiles_of)]
         mean_var = [held.tile([P, tiles, 2], F32, name=f"mean_var{c}") for c, tiles in enumerate(tiles_of)]
-        var_eps = [held.tile([P, tiles, 1], F32, name=f"var_eps{c}") for c, tiles in enumerate(tiles_of)]
         rstd = [held.tile([P, tiles, 1], F32, name=f"rstd{c}") for c, tiles in enumerate(tiles_of)]
         normed = held.tile([P, TOKEN_TILES, C], F32, name="normed")
         per_partition = held.tile([P, COLS_USED], F32, name="per_partition")
@@ -98,13 +102,17 @@ def tile_multiheadefralayer_kernel(tc, base, h, ln_gain, ln_bias, w1, b1, w2, b2
                 for blk in range(C_BLOCKS):
                     nc.tensor.transpose(h_flipped[chunk][:, i, blk * P : (blk + 1) * P], h_sb[blk][:, tokens], identity[:])
 
-        def moments(chunk):
+        def moments(chunk, root_engine):
             for i in range(tiles_of[chunk]):
                 nc.vector.bn_stats(stats[chunk][:, i, :], h_flipped[chunk][:, i, :])
             for i in range(tiles_of[chunk]):
                 nc.vector.bn_aggr(mean_var[chunk][:, i, :], stats[chunk][:, i, :])
-            nc.vector.tensor_scalar_add(var_eps[chunk][:], mean_var[chunk][:, :, 1:2], EPS)
-            nc.gpsimd.tensor_tensor(rstd[chunk][:], var_eps[chunk][:], minus_half[:, 0 : tiles_of[chunk], :], ALU.pow)
+            if root_engine == "scalar":
+                nc.scalar.activation(rstd[chunk][:], mean_var[chunk][:, :, 1:2], ACT.Abs_reciprocal_sqrt, bias=eps[:])
+            else:
+                var_eps = held.tile([P, tiles_of[chunk], 1], F32, name=f"var_eps{chunk}")
+                nc.vector.tensor_scalar_add(var_eps[:], mean_var[chunk][:, :, 1:2], EPS)
+                nc.gpsimd.tensor_tensor(rstd[chunk][:], var_eps[:], minus_half[:, 0 : tiles_of[chunk], :], ALU.pow)
 
         def normalise(chunk):
             first, size = CHUNKS[chunk]
@@ -159,34 +167,35 @@ def tile_multiheadefralayer_kernel(tc, base, h, ln_gain, ln_bias, w1, b1, w2, b2
         lower = range(0, F_BLOCKS // 2)
         upper = range(F_BLOCKS // 2, F_BLOCKS)
         flip_in(0)
-        moments(0)
+        moments(0, "scalar")
         flip_in(1)
-        moments(1)
+        moments(1, "scalar")
         flip_in(2)
-        moments(2)
         flip_small_vectors()
-        flip_in(3)
-        flip_in(4)
         normalise(0)
         normalise(1)
+        flip_in(3)
         gain_and_bias(0, "scalar")
-        gain_and_bias(1, "scalar")
+        moments(2, "scalar")
+        change_to_gelu_table(rstd[2][:, 0, :])
+        gain_and_bias(1, "vector")
+        flip_in(4)
         first_matmul(0, lower)
         normalise(2)
         first_matmul(0, upper)
-        moments(3)
+        moments(3, "gpsimd")
         gain_and_bias(2, "vector")
         first_matmul(1, lower)
         first_matmul(1, upper)
-        moments(4)
         first_matmul(2, lower)
         normalise(3)
+        moments(4, "gpsimd")
         first_matmul(2, upper)
-        normalise(4)
         gain_and_bias(3, "vector")
-        gain_and_bias(4, "vector")
         first_matmul(3, lower)
+        normalise(4)
         first_matmul(3, upper)
+        gain_and_bias(4, "vector")
         first_matmul(4, lower)
         first_matmul(4, upper)
 

@@ -172,9 +172,9 @@ def tile_multiheadefralayer_kernel(tc, base, h, ln_gain, ln_bias, w1, b1, w2, b2
         moments(1, "scalar")
         flip_in(2)
         flip_small_vectors()
+        flip_in(3)
         normalise(0)
         normalise(1)
-        flip_in(3)
         gain_and_bias(0, "scalar")
         moments(2, "scalar")
         change_to_gelu_table(rstd[2][:, 0, :])

@@ -18,7 +18,8 @@ BANK = 512
 C_BLOCKS = C // P
 F_BLOCKS = F // P
 TOKEN_TILES = N // P
-Y_PIECE = 256
+Y_PIECES = (256, 256, 256, 128, 128)
+assert sum(Y_PIECES) == N
 CHUNKS = ((0, 128), (128, 128), (256, 256), (512, 256), (768, 256))
 MAX_TILES = 2
 
@@ -201,9 +202,9 @@ def tile_multiheadefralayer_kernel(tc, base, h, ln_gain, ln_bias, w1, b1, w2, b2
 
         y_sb = [held.tile([P, N], F32, name=f"y{blk}") for blk in range(C_BLOCKS)]
         for blk in range(C_BLOCKS):
-            for piece in range(N // Y_PIECE):
-                tokens = slice(piece * Y_PIECE, (piece + 1) * Y_PIECE)
-                y = banks.tile([P, Y_PIECE], F32, name="y", tag="bank")
+            for piece, size in enumerate(Y_PIECES):
+                tokens = slice(sum(Y_PIECES[:piece]), sum(Y_PIECES[:piece]) + size)
+                y = banks.tile([P, size], F32, name="y", tag="bank")
                 for k in range(F_BLOCKS):
                     nc.tensor.matmul(
                         y[:],
@@ -212,8 +213,10 @@ def tile_multiheadefralayer_kernel(tc, base, h, ln_gain, ln_bias, w1, b1, w2, b2
                         start=(k == 0),
                         stop=(k == F_BLOCKS - 1),
                     )
-                nc.scalar.activation(
-                    y_sb[blk][:, tokens], y[:], ACT.Identity, bias=per_partition[:, COL_B2 + blk : COL_B2 + blk + 1]
-                )
+                b2_column = per_partition[:, COL_B2 + blk : COL_B2 + blk + 1]
+                if blk == 0:
+                    nc.vector.tensor_scalar_add(y_sb[blk][:, tokens], y[:], b2_column)
+                else:
+                    nc.scalar.activation(y_sb[blk][:, tokens], y[:], ACT.Identity, bias=b2_column)
             nc.vector.tensor_tensor(window[blk][:].indirect(offsets[:]), h_sb[blk][:], y_sb[blk][:], ALU.add)
             nc.sync.dma_start(out[blk * P : (blk + 1) * P, :], window[blk][:])

@@ -47,12 +47,12 @@ def tile_multiheadefralayer_kernel(tc, base, h, ln_gain, ln_bias, w1, b1, w2, b2
         rows = held.tile([P, P], F32, name="rows")
         nc.vector.memset(rows[:], 0.0)
 
-        h_sb = [held.tile([P, N], F32, name=f"h{blk}") for blk in range(C_BLOCKS)]
+        h_all = held.tile([P, C_BLOCKS, N], F32, name="h_all")
+        h_by_block = h.rearrange("(blk p) n -> p blk n", p=P)
 
         def load_h(chunk):
             first, size = CHUNKS[chunk]
-            for blk in range(C_BLOCKS):
-                nc.sync.dma_start(h_sb[blk][:, first : first + size], h[blk * P : (blk + 1) * P, first : first + size])
+            nc.sync.dma_start(h_all[:, :, first : first + size], h_by_block[:, :, first : first + size])
 
         load_h(0)
         load_h(1)
@@ -62,9 +62,8 @@ def tile_multiheadefralayer_kernel(tc, base, h, ln_gain, ln_bias, w1, b1, w2, b2
             nc.sync.dma_start(rows[first_row : first_row + as_rows.shape[0], :], as_rows)
         load_h(3)
         load_h(4)
-        w1_sb = [held.tile([P, F], BF16, name=f"w1_{blk}") for blk in range(C_BLOCKS)]
-        for blk in range(C_BLOCKS):
-            nc.sync.dma_start(w1_sb[blk][:], w1[blk * P : (blk + 1) * P, :])
+        w1_all = held.tile([P, C_BLOCKS, F], BF16, name="w1_all")
+        nc.sync.dma_start(w1_all[:], w1.rearrange("(blk p) f -> p blk f", p=P))
         w2_sb = held.tile([P, F_BLOCKS, C], BF16, name="w2_sb")
         nc.sync.dma_start(w2_sb[:], w2.rearrange("(k p) c -> p k c", p=P))
         offsets = held.tile([P, N // 16], U16, name="offsets")
@@ -101,7 +100,7 @@ def tile_multiheadefralayer_kernel(tc, base, h, ln_gain, ln_bias, w1, b1, w2, b2
             for i in range(tiles_of[chunk]):
                 tokens = slice(first + i * P, first + (i + 1) * P)
                 for blk in range(C_BLOCKS):
-                    nc.tensor.transpose(h_flipped[chunk][:, i, blk * P : (blk + 1) * P], h_sb[blk][:, tokens], identity[:])
+                    nc.tensor.transpose(h_flipped[chunk][:, i, blk * P : (blk + 1) * P], h_all[:, blk, tokens], identity[:])
 
         def moments(chunk, root_engine):
             for i in range(tiles_of[chunk]):
@@ -154,7 +153,7 @@ def tile_multiheadefralayer_kernel(tc, base, h, ln_gain, ln_bias, w1, b1, w2, b2
                     for k in range(C_BLOCKS):
                         nc.tensor.matmul(
                             z[:, i, :],
-                            w1_sb[k][:, (lowest + i) * P : (lowest + i + 1) * P],
+                            w1_all[:, k, (lowest + i) * P : (lowest + i + 1) * P],
                             x_sb[k][:, tokens],
                             start=(k == 0),
                             stop=(k == C_BLOCKS - 1),
@@ -218,5 +217,5 @@ def tile_multiheadefralayer_kernel(tc, base, h, ln_gain, ln_bias, w1, b1, w2, b2
                     nc.vector.tensor_scalar_add(y_sb[blk][:, tokens], y[:], b2_column)
                 else:
                     nc.scalar.activation(y_sb[blk][:, tokens], y[:], ACT.Identity, bias=b2_column)
-            nc.vector.tensor_tensor(window[blk][:].indirect(offsets[:]), h_sb[blk][:], y_sb[blk][:], ALU.add)
+            nc.vector.tensor_tensor(window[blk][:].indirect(offsets[:]), h_all[:, blk, :], y_sb[blk][:], ALU.add)
             nc.sync.dma_start(out[blk * P : (blk + 1) * P, :], window[blk][:])

@@ -75,8 +75,8 @@ def tile_multiheadefralayer_kernel(tc, base, h, ln_gain, ln_bias, w1, b1, w2, b2
         table_warmer = held.tile([P, 2], F32, name="table_warmer")
         nc.scalar.activation(table_warmer[:, 0:1], eps[:], ACT.Abs_reciprocal_sqrt)
 
-        def change_to_gelu_table(last_root):
-            nc.scalar.activation(table_warmer[:, 1:2], last_root, ACT.Gelu)
+        def change_to_gelu_table(last_root, last_x):
+            nc.scalar.activation(table_warmer[:, 1:2], last_root, ACT.Gelu, bias=last_x)
 
         tiles_of = [size // P for first, size in CHUNKS]
         stats = [held.tile([P, tiles, 6], F32, name=f"stats{c}") for c, tiles in enumerate(tiles_of)]
@@ -94,17 +94,21 @@ def tile_multiheadefralayer_kernel(tc, base, h, ln_gain, ln_bias, w1, b1, w2, b2
             nc.tensor.transpose(flipped_rows[:, 0:P], rows[:], identity[:])
             nc.scalar.copy(per_partition[:], flipped_rows[:, 0:COLS_USED])
 
-        def flip_in(chunk):
+        def flip_in(chunk, tiles_in_a_bank):
             first, size = CHUNKS[chunk]
-            h_flipped[chunk] = banks.tile([P, tiles_of[chunk], C], F32, name=f"h_flipped{chunk}", tag="bank")
             for i in range(tiles_of[chunk]):
-                tokens = slice(first + i * P, first + (i + 1) * P)
+                t = first // P + i
+                if i % tiles_in_a_bank == 0:
+                    bank = banks.tile([P, tiles_in_a_bank, C], F32, name=f"h_flipped{t}", tag="bank")
+                place = i % tiles_in_a_bank
+                h_flipped[t] = (bank, place)
                 for blk in range(C_BLOCKS):
-                    nc.tensor.transpose(h_flipped[chunk][:, i, blk * P : (blk + 1) * P], h_all[:, blk, tokens], identity[:])
+                    nc.tensor.transpose(bank[:, place, blk * P : (blk + 1) * P], h_all[:, blk, t * P : (t + 1) * P], identity[:])
 
         def moments(chunk, root_engine):
             for i in range(tiles_of[chunk]):
-                nc.vector.bn_stats(stats[chunk][:, i, :], h_flipped[chunk][:, i, :])
+                bank, place = h_flipped[CHUNKS[chunk][0] // P + i]
+                nc.vector.bn_stats(stats[chunk][:, i, :], bank[:, place, :])
             for i in range(tiles_of[chunk]):
                 nc.vector.bn_aggr(mean_var[chunk][:, i, :], stats[chunk][:, i, :])
             if root_engine == "scalar":
@@ -116,20 +120,26 @@ def tile_multiheadefralayer_kernel(tc, base, h, ln_gain, ln_bias, w1, b1, w2, b2
 
         def normalise(chunk):
             first, size = CHUNKS[chunk]
-            back[chunk] = banks.tile([P, C_BLOCKS, size], F32, name=f"back{chunk}", tag="bank")
             for i in range(tiles_of[chunk]):
-                t = first // P + i
+                bank, place = h_flipped[first // P + i]
                 nc.vector.tensor_scalar(
-                    normed[:, t, :],
-                    h_flipped[chunk][:, i, :],
+                    normed[:, first // P + i, :],
+                    bank[:, place, :],
                     mean_var[chunk][:, i, 0:1],
                     rstd[chunk][:, i, :],
                     ALU.subtract,
                     ALU.mult,
                 )
+
+        def flip_back(chunk):
+            first, size = CHUNKS[chunk]
+            back[chunk] = banks.tile([P, C_BLOCKS, size], F32, name=f"back{chunk}", tag="bank")
+            for i in range(tiles_of[chunk]):
                 for blk in range(C_BLOCKS):
                     nc.tensor.transpose(
-                        back[chunk][:, blk, i * P : (i + 1) * P], normed[:, t, blk * P : (blk + 1) * P], identity[:]
+                        back[chunk][:, blk, i * P : (i + 1) * P],
+                        normed[:, first // P + i, blk * P : (blk + 1) * P],
+                        identity[:],
                     )
 
         def gain_and_bias(chunk, engine):
@@ -166,34 +176,39 @@ def tile_multiheadefralayer_kernel(tc, base, h, ln_gain, ln_bias, w1, b1, w2, b2
 
         lower = range(0, F_BLOCKS // 2)
         upper = range(F_BLOCKS // 2, F_BLOCKS)
-        flip_in(0)
+        flip_in(0, 1)
         moments(0, "scalar")
-        flip_in(1)
+        flip_in(1, 1)
         moments(1, "scalar")
-        flip_in(2)
+        flip_in(2, 1)
         flip_small_vectors()
-        flip_in(3)
+        flip_in(3, 2)
         normalise(0)
+        flip_back(0)
         normalise(1)
+        flip_back(1)
         gain_and_bias(0, "scalar")
         moments(2, "scalar")
-        change_to_gelu_table(rstd[2][:, 0, :])
-        gain_and_bias(1, "vector")
-        flip_in(4)
-        first_matmul(0, lower)
+        moments(3, "scalar")
+        change_to_gelu_table(rstd[3][:, 0, :], x_sb[C_BLOCKS - 1][:, 0:1])
         normalise(2)
+        gain_and_bias(1, "vector")
+        flip_in(4, 2)
+        first_matmul(0, lower)
+        flip_back(2)
         first_matmul(0, upper)
-        moments(3, "gpsimd")
+        moments(4, "gpsimd")
         gain_and_bias(2, "vector")
         first_matmul(1, lower)
         first_matmul(1, upper)
-        first_matmul(2, lower)
         normalise(3)
-        moments(4, "gpsimd")
+        normalise(4)
+        first_matmul(2, lower)
+        flip_back(3)
         first_matmul(2, upper)
         gain_and_bias(3, "vector")
         first_matmul(3, lower)
-        normalise(4)
+        flip_back(4)
         first_matmul(3, upper)
         gain_and_bias(4, "vector")
         first_matmul(4, lower)

import concourse.mybir as mybir
from concourse.masks import make_identity

F32 = mybir.dt.float32
BF16 = mybir.dt.bfloat16
U16 = mybir.dt.uint16
ACT = mybir.ActivationFunctionType
ALU = mybir.AluOpType

P = 128
C = 256
F = 1024
S = 2048
N = 1024
EPS = 1e-5
BANK = 512

C_BLOCKS = C // P
F_BLOCKS = F // P
TOKEN_TILES = N // P
Y_PIECES = (256, 256, 256, 128, 128)
assert sum(Y_PIECES) == N
CHUNKS = ((0, 128), (128, 128), (256, 256), (512, 256), (768, 256))
MAX_TILES = 2

COL_B1 = 0
COL_GAIN = COL_B1 + F_BLOCKS
COL_BIAS = COL_GAIN + C_BLOCKS
COL_B2 = COL_BIAS + C_BLOCKS
COLS_USED = COL_B2 + C_BLOCKS

FLOPS = 2 * C * F * N * 2


def tile_multiheadefralayer_kernel(tc, base, h, ln_gain, ln_bias, w1, b1, w2, b2, offs, out):
    nc = tc.nc
    with (
        tc.tile_pool(name="held", bufs=1) as held,
        tc.psum_pool(name="banks", bufs=8) as banks,
    ):
        identity = held.tile([P, P], F32, name="identity")
        make_identity(nc, identity[:])
        minus_half = held.tile([P, MAX_TILES, 1], F32, name="minus_half")
        nc.vector.memset(minus_half[:], -0.5)
        eps = held.tile([P, 1], F32, name="eps")
        nc.vector.memset(eps[:], EPS)
        rows = held.tile([P, P], F32, name="rows")
        nc.vector.memset(rows[:], 0.0)

        h_all = held.tile([P, C_BLOCKS, N], F32, name="h_all")
        h_by_block = h.rearrange("(blk p) n -> p blk n", p=P)

        def load_h(chunk):
            first, size = CHUNKS[chunk]
            nc.sync.dma_start(h_all[:, :, first : first + size], h_by_block[:, :, first : first + size])

        load_h(0)
        load_h(1)
        load_h(2)
        for vector, first_row in ((b1, COL_B1), (ln_gain, COL_GAIN), (ln_bias, COL_BIAS), (b2, COL_B2)):
            as_rows = vector.rearrange("(r p) one -> r (p one)", p=P)
            nc.sync.dma_start(rows[first_row : first_row + as_rows.shape[0], :], as_rows)
        load_h(3)
        load_h(4)
        w1_all = held.tile([P, C_BLOCKS, F], BF16, name="w1_all")
        nc.sync.dma_start(w1_all[:], w1.rearrange("(blk p) f -> p blk f", p=P))
        w2_sb = held.tile([P, F_BLOCKS, C], BF16, name="w2_sb")
        nc.sync.dma_start(w2_sb[:], w2.rearrange("(k p) c -> p k c", p=P))
        offsets = held.tile([P, N // 16], U16, name="offsets")
        nc.sync.dma_start(offsets[:], offs)
        window = [held.tile([P, S], F32, name=f"window{blk}") for blk in range(C_BLOCKS)]
        for blk in range(C_BLOCKS):
            nc.sync.dma_start(window[blk][:], base[blk * P : (blk + 1) * P, :])

        table_warmer = held.tile([P, 2], F32, name="table_warmer")
        nc.scalar.activation(table_warmer[:, 0:1], eps[:], ACT.Abs_reciprocal_sqrt)

        def change_to_gelu_table(last_root, last_x):
            nc.scalar.activation(table_warmer[:, 1:2], last_root, ACT.Gelu, bias=last_x)

        tiles_of = [size // P for first, size in CHUNKS]
        stats = [held.tile([P, tiles, 6], F32, name=f"stats{c}") for c, tiles in enumerate(tiles_of)]
        mean_var = [held.tile([P, tiles, 2], F32, name=f"mean_var{c}") for c, tiles in enumerate(tiles_of)]
        rstd = [held.tile([P, tiles, 1], F32, name=f"rstd{c}") for c, tiles in enumerate(tiles_of)]
        normed = held.tile([P, TOKEN_TILES, C], F32, name="normed")
        per_partition = held.tile([P, COLS_USED], F32, name="per_partition")
        x_sb = [held.tile([P, N], BF16, name=f"x{blk}") for blk in range(C_BLOCKS)]
        a_sb = held.tile([P, F_BLOCKS, N], BF16, name="a_sb")
        h_flipped = {}
        back = {}

        def flip_small_vectors():
            flipped_rows = banks.tile([P, BANK], F32, name="flipped_rows", tag="bank")
            nc.tensor.transpose(flipped_rows[:, 0:P], rows[:], identity[:])
            nc.scalar.copy(per_partition[:], flipped_rows[:, 0:COLS_USED])

        def flip_in(chunk, tiles_in_a_bank):
            first, size = CHUNKS[chunk]
            for i in range(tiles_of[chunk]):
                t = first // P + i
                if i % tiles_in_a_bank == 0:
                    bank = banks.tile([P, tiles_in_a_bank, C], F32, name=f"h_flipped{t}", tag="bank")
                place = i % tiles_in_a_bank
                h_flipped[t] = (bank, place)
                for blk in range(C_BLOCKS):
                    nc.tensor.transpose(bank[:, place, blk * P : (blk + 1) * P], h_all[:, blk, t * P : (t + 1) * P], identity[:])

        def moments(chunk, root_engine):
            for i in range(tiles_of[chunk]):
                bank, place = h_flipped[CHUNKS[chunk][0] // P + i]
                nc.vector.bn_stats(stats[chunk][:, i, :], bank[:, place, :])
            for i in range(tiles_of[chunk]):
                nc.vector.bn_aggr(mean_var[chunk][:, i, :], stats[chunk][:, i, :])
            if root_engine == "scalar":
                nc.scalar.activation(rstd[chunk][:], mean_var[chunk][:, :, 1:2], ACT.Abs_reciprocal_sqrt, bias=eps[:])
            else:
                var_eps = held.tile([P, tiles_of[chunk], 1], F32, name=f"var_eps{chunk}")
                nc.vector.tensor_scalar_add(var_eps[:], mean_var[chunk][:, :, 1:2], EPS)
                nc.gpsimd.tensor_tensor(rstd[chunk][:], var_eps[:], minus_half[:, 0 : tiles_of[chunk], :], ALU.pow)

        def normalise(chunk):
            first, size = CHUNKS[chunk]
            for i in range(tiles_of[chunk]):
                bank, place = h_flipped[first // P + i]
                nc.vector.tensor_scalar(
                    normed[:, first // P + i, :],
                    bank[:, place, :],
                    mean_var[chunk][:, i, 0:1],
                    rstd[chunk][:, i, :],
                    ALU.subtract,
                    ALU.mult,
                )

        def flip_back(chunk):
            first, size = CHUNKS[chunk]
            back[chunk] = banks.tile([P, C_BLOCKS, size], F32, name=f"back{chunk}", tag="bank")
            for i in range(tiles_of[chunk]):
                for blk in range(C_BLOCKS):
                    nc.tensor.transpose(
                        back[chunk][:, blk, i * P : (i + 1) * P],
                        normed[:, first // P + i, blk * P : (blk + 1) * P],
                        identity[:],
                    )

        def gain_and_bias(chunk, engine):
            first, size = CHUNKS[chunk]
            for blk in range(C_BLOCKS):
                x_chunk = x_sb[blk][:, first : first + size]
                gain = per_partition[:, COL_GAIN + blk : COL_GAIN + blk + 1]
                bias = per_partition[:, COL_BIAS + blk : COL_BIAS + blk + 1]
                if engine == "scalar":
                    nc.scalar.activation(x_chunk, back[chunk][:, blk, :], ACT.Identity, bias=bias, scale=gain)
                else:
                    nc.vector.tensor_scalar(x_chunk, back[chunk][:, blk, :], gain, bias, ALU.mult, ALU.add)

        def first_matmul(chunk, feature_blocks):
            first, size = CHUNKS[chunk]
            tokens = slice(first, first + size)
            per_bank = BANK // size
            for lowest in feature_blocks[0::per_bank]:
                z = banks.tile([P, per_bank, size], F32, name="z", tag="bank")
                for i in range(per_bank):
                    for k in range(C_BLOCKS):
                        nc.tensor.matmul(
                            z[:, i, :],
                            w1_all[:, k, (lowest + i) * P : (lowest + i + 1) * P],
                            x_sb[k][:, tokens],
                            start=(k == 0),
                            stop=(k == C_BLOCKS - 1),
                        )
                for i in range(per_bank):
                    m = lowest + i
                    nc.scalar.activation(
                        a_sb[:, m, tokens], z[:, i, :], ACT.Gelu, bias=per_partition[:, COL_B1 + m : COL_B1 + m + 1]
                    )

        lower = range(0, F_BLOCKS // 2)
        upper = range(F_BLOCKS // 2, F_BLOCKS)
        flip_in(0, 1)
        moments(0, "scalar")
        flip_in(1, 1)
        moments(1, "scalar")
        flip_in(2, 1)
        flip_small_vectors()
        flip_in(3, 2)
        normalise(0)
        flip_back(0)
        normalise(1)
        flip_back(1)
        gain_and_bias(0, "scalar")
        moments(2, "scalar")
        moments(3, "scalar")
        change_to_gelu_table(rstd[3][:, 0, :], x_sb[C_BLOCKS - 1][:, 0:1])
        normalise(2)
        gain_and_bias(1, "vector")
        flip_in(4, 2)
        first_matmul(0, lower)
        flip_back(2)
        first_matmul(0, upper)
        moments(4, "gpsimd")
        gain_and_bias(2, "vector")
        first_matmul(1, lower)
        first_matmul(1, upper)
        normalise(3)
        normalise(4)
        first_matmul(2, lower)
        flip_back(3)
        first_matmul(2, upper)
        gain_and_bias(3, "vector")
        first_matmul(3, lower)
        flip_back(4)
        first_matmul(3, upper)
        gain_and_bias(4, "vector")
        first_matmul(4, lower)
        first_matmul(4, upper)

        y_sb = [held.tile([P, N], F32, name=f"y{blk}") for blk in range(C_BLOCKS)]
        for blk in range(C_BLOCKS):
            for piece, size in enumerate(Y_PIECES):
                tokens = slice(sum(Y_PIECES[:piece]), sum(Y_PIECES[:piece]) + size)
                y = banks.tile([P, size], F32, name="y", tag="bank")
                for k in range(F_BLOCKS):
                    nc.tensor.matmul(
                        y[:],
                        w2_sb[:, k, blk * P : (blk + 1) * P],
                        a_sb[:, k, tokens],
                        start=(k == 0),
                        stop=(k == F_BLOCKS - 1),
                    )
                b2_column = per_partition[:, COL_B2 + blk : COL_B2 + blk + 1]
                if blk == 0:
                    nc.vector.tensor_scalar_add(y_sb[blk][:, tokens], y[:], b2_column)
                else:
                    nc.scalar.activation(y_sb[blk][:, tokens], y[:], ACT.Identity, bias=b2_column)
            nc.vector.tensor_tensor(window[blk][:].indirect(offsets[:]), h_all[:, blk, :], y_sb[blk][:], ALU.add)
            nc.sync.dma_start(out[blk * P : (blk + 1) * P, :], window[blk][:])
